import numpy as np
import ml_dtypes


def mxq(x, axis, fmt="e4m3"):
    dtype, down = {"e4m3": (ml_dtypes.float8_e4m3fn, 7), "e5m2": (ml_dtypes.float8_e5m2, 14)}[fmt]
    v = np.moveaxis(np.asarray(x, np.float32).astype(ml_dtypes.bfloat16).astype(np.float64), axis, -1)
    blocks = v.reshape(v.shape[:-1] + (-1, 32))
    amax = np.abs(blocks).max(-1, keepdims=True)
    byte = np.maximum(np.where(amax > 0, np.frexp(amax)[1] - 1 + 127, 0) - down, 1)
    scale = np.exp2(byte - 127.0)
    codes = (blocks / scale).astype(np.float32).astype(dtype).astype(np.float64)
    return np.moveaxis((codes * scale).reshape(v.shape), -1, axis)


WIDE = False


def mx_kscale(k):
    if not WIDE:
        return np.ones(k)
    levels = np.array([10, -10, 5, -5, 0])
    a = np.random.permutation(np.resize(levels, k // 512 * 4)).reshape(k // 512, 4)
    idx = np.arange(k)
    return np.exp2(a[idx // 512, idx % 128 // 32])


BF16 = ml_dtypes.bfloat16


def bf(x):
    return np.asarray(x, np.float32).astype(BF16)


def f64(x):
    return np.asarray(x).astype(np.float64)


E2M1 = np.array([0.0, 0.5, 1.0, 1.5, 2.0, 3.0, 4.0, 6.0, -0.0, -0.5, -1.0, -1.5, -2.0, -3.0, -4.0, -6.0])


def pack_weight(w, fmt):
    k, n = w.shape
    w = f64(bf(w)).reshape(k // 32, 32, n)
    amax = np.abs(w).max(1)
    if fmt == "e4m3":
        byte = np.frexp(amax)[1] - 1 + 127 - 7
    else:
        mant, ex = np.frexp(amax / 6.0)
        byte = np.where(mant > 0.5, ex, ex - 1) + 127
    byte = np.clip(np.where(amax > 0, byte, 1), 1, 254)
    scaled = (w * np.exp2(127.0 - byte)[:, None, :]).reshape(k, n).astype(np.float32)
    by_word = np.ascontiguousarray(scaled.reshape(k // 512, 128, 4, n).transpose(0, 1, 3, 2))
    if fmt == "e4m3":
        words = by_word.astype(ml_dtypes.float8_e4m3fn).view(np.uint8)
    else:
        c = by_word.astype(ml_dtypes.float4_e2m1fn).view(np.uint8) & 0xF
        words = c[..., 0::2] | (c[..., 1::2] << 4)
    return np.ascontiguousarray(words), np.ascontiguousarray(byte.astype(np.uint8).reshape(k // 512, 16, n))


def unpack_weight(words, scales, fmt):
    g, p, n, _ = words.shape
    if fmt == "e4m3":
        vals = np.ascontiguousarray(words).view(ml_dtypes.float8_e4m3fn).astype(np.float64)
    else:
        nib = np.empty((g, p, n, 4), np.uint8)
        nib[..., 0::2] = words & 0xF
        nib[..., 1::2] = words >> 4
        vals = E2M1[nib]
    vals = vals * np.repeat(np.exp2(scales.astype(np.float64) - 127.0), 8, axis=1)[..., None]
    return vals.transpose(0, 1, 3, 2).reshape(g * 512, n)


B, IN, HID, N, NM = 2, 128, 384, 512, 5
C = IN + HID
K = NM * C


def setup_inputs():
    t = mx_kscale(C)
    tc = t[None, :, None]
    x_cand = bf(np.random.standard_normal((B, C, N)) * 0.8 * tc)
    x1_0 = bf(np.random.standard_normal((B, C, N)) * 0.55 * tc)
    x1_1 = bf(np.random.standard_normal((B, C, N)) * 0.55 * tc)
    support0 = bf(np.random.standard_normal((N, N)) * 0.7 / np.sqrt(N))
    support1 = bf(np.random.standard_normal((N, N)) * 0.7 / np.sqrt(N))
    words, scales = pack_weight(np.random.standard_normal((K, HID)) / np.sqrt(K) / np.tile(t, NM)[:, None], "e4m3")
    b_c = bf(0.3 * np.random.standard_normal(HID))
    u = bf(1.0 / (1.0 + np.exp(-(1.0 + np.random.standard_normal((B, HID, N))))))
    hx = bf(np.random.standard_normal((B, HID, N)))
    return {"x_cand": x_cand,
            "x1_0": x1_0,
            "x1_1": x1_1,
            "support0": support0,
            "support1": support1,
            "W_c_words": words,
            "W_c_scales": scales,
            "b_c": b_c,
            "u": u,
            "hx": hx}


def reference(x_cand, x1_0, x1_1, support0, support1, W_c_words, W_c_scales, b_c, u, hx):
    x0, xa, xb = f64(x_cand), f64(x1_0), f64(x1_1)
    x2a = 2.0 * (mxq(xa, 2, "e4m3") @ mxq(f64(support0).T, 0, "e4m3")) - x0
    x2b = 2.0 * (mxq(xb, 2, "e4m3") @ mxq(f64(support1).T, 0, "e4m3")) - x0
    h = np.concatenate([x0, xa, x2a, xb, x2b], axis=1)
    cand = np.tanh((unpack_weight(W_c_words, W_c_scales, "e4m3").T @ mxq(h, 1, "e4m3")) + f64(b_c)[None, :, None])
    return f64(u) * f64(hx) + (1.0 - f64(u)) * cand

@@ -1,0 +1,253 @@
+from contextlib import ExitStack
+
+import concourse.mybir as mybir
+from concourse.masks import make_identity
+
+F32 = mybir.dt.float32
+BF16 = mybir.dt.bfloat16
+I32 = mybir.dt.int32
+U32 = mybir.dt.uint32
+U8 = mybir.dt.uint8
+FP8X4 = mybir.dt.float8_e4m3fn_x4
+ALU = mybir.AluOpType
+ACT = mybir.ActivationFunctionType
+
+P = 128
+PACK = 4
+BATCH = 2
+CHANNELS = P * PACK
+NODES = 512
+NODE_TILES = NODES // P
+HID = 384
+HID_TILES = HID // P
+BLOCKS = 5
+X_CAND, X1_BLOCK, X2_BLOCK = 0, (1, 3), (2, 4)
+BLOCK_ORDER = (0, 2, 4, 1, 3)
+STEPS = tuple((b, s) for b in range(BATCH) for s in range(2))
+
+FLOPS = 2 * 2 * BATCH * CHANNELS * NODES * NODES + 2 * BATCH * BLOCKS * CHANNELS * HID * NODES
+
+
+def tile_dcgrucell_pc_kernel(
+    tc, x_cand, x1_0, x1_1, support0, support1, W_c_words, W_c_scales, b_c, u, hx, out
+):
+    nc = tc.nc
+    x1 = (x1_0, x1_1)
+    support = (support0, support1)
+
+    with ExitStack() as ctx:
+        ctx.enter_context(tc.manual_schedule())
+        keep = ctx.enter_context(tc.tile_pool(name="keep", bufs=1))
+        blend_pool = ctx.enter_context(tc.tile_pool(name="blend_pool", bufs=HID_TILES))
+        psum = ctx.enter_context(tc.psum_pool(name="psum", bufs=8))
+
+        w_scales = keep.tile([P, BLOCKS, HID], U8, align_bytes=64)
+        nc.vector.memset(w_scales[:].rearrange("p g o -> p (g o)").bitcast(I32), 0)
+        ident = keep.tile([P, P], F32)
+        make_identity(nc, ident[:])
+        for quadrant in range(4):
+            nc.gpsimd.dma_start(
+                out=w_scales[32 * quadrant : 32 * quadrant + 4, :, :].bitcast(F32),
+                in_=W_c_scales[:, 4 * quadrant : 4 * quadrant + 4, :]
+                .rearrange("g r o -> r g o")
+                .bitcast(F32),
+            )
+        zero_column = keep.tile([P, 1], F32)
+        nc.vector.memset(zero_column[:], 0.0)
+        table_warmer = keep.tile([P, 1], F32)
+        nc.scalar.activation(out=table_warmer[:], in_=zero_column[:], func=ACT.Tanh)
+
+        def load_channels(src, name):
+            by_four = keep.tile([P, PACK, NODES], BF16, name=name)
+            nc.sync.dma_start(out=by_four[:], in_=src.rearrange("(p j) n -> p j n", j=PACK))
+            return by_four
+
+        def load_support(s):
+            rows = keep.tile([P, NODE_TILES, NODES], BF16, name="support_sb%d" % s)
+            nc.sync.dma_start(out=rows[:], in_=support[s].rearrange("(r p) n -> p r n", p=P))
+            return rows
+
+        def load_hidden(src, name):
+            rows = keep.tile([P, HID_TILES, NODES], BF16, name=name)
+            nc.sync.dma_start(out=rows[:], in_=src.rearrange("(i p) n -> p i n", p=P))
+            return rows
+
+        bias_bf16 = keep.tile([HID_TILES, P], BF16)
+        nc.sync.dma_start(out=bias_bf16[:], in_=b_c.rearrange("(i p) -> i p", p=P))
+        support_sb, x0_sb, x1_sb, u_sb, hx_sb = {}, {}, {}, {}, {}
+        support_sb[0] = load_support(0)
+        x1_sb[0, 0] = load_channels(x1[0][0], "x1_sb00")
+        x0_sb[0] = load_channels(x_cand[0], "x0_sb0")
+        support_sb[1] = load_support(1)
+        x1_sb[0, 1] = load_channels(x1[1][0], "x1_sb01")
+        x1_sb[1, 0] = load_channels(x1[0][1], "x1_sb10")
+        x1_sb[1, 1] = load_channels(x1[1][1], "x1_sb11")
+        x0_sb[1] = load_channels(x_cand[1], "x0_sb1")
+        w_codes = keep.tile([P, BLOCKS, HID], U32, align_bytes=64)
+        nc.sync.dma_start(
+            out=w_codes[:].bitcast(I32),
+            in_=W_c_words.rearrange("g p o t -> p g (o t)").bitcast(I32),
+        )
+        for b in range(BATCH):
+            u_sb[b] = load_hidden(u[b], "u_sb%d" % b)
+            hx_sb[b] = load_hidden(hx[b], "hx_sb%d" % b)
+
+        bias_rows = keep.tile([P, P], F32)
+        nc.vector.memset(bias_rows[:], 0.0)
+        nc.vector.tensor_copy(out=bias_rows[0:HID_TILES, :], in_=bias_bf16[:])
+        bias_bank = psum.tile([P, P], F32, tag="bank")
+        nc.tensor.transpose(bias_bank[:], bias_rows[:], ident[:])
+        bias = keep.tile([P, HID_TILES], F32)
+        nc.vector.tensor_copy(out=bias[:], in_=bias_bank[:, 0:HID_TILES])
+
+        mx = {}
+
+        def new_grouped(name):
+            return keep.tile([P, NODES, PACK], BF16, name=name + "_grouped", align_bytes=64)
+
+        def quantise(name, grouped):
+            codes = keep.tile([P, NODES], U32, name=name + "_codes", align_bytes=64)
+            scales = keep.tile([P, NODES], U8, name=name + "_scales", align_bytes=64)
+            nc.vector.quantize_mx(
+                out=codes[:].bitcast(FP8X4),
+                scales=scales[:],
+                in_=grouped[:].rearrange("p c t -> p (c t)"),
+            )
+            mx[name] = (codes, scales)
+
+        def nodes_to_partitions(rows_sb, name, second_copy):
+            words = rows_sb[:].bitcast(F32)
+            grouped = new_grouped(name)
+            grouped_words = grouped[:].bitcast(F32).rearrange("q (a r) v -> q a r v", r=P)
+            for pair, copy in enumerate((nc.scalar.copy, second_copy)):
+                flipped = psum.tile([P, 2, 2, P], F32, tag="bank")
+                for a in range(2):
+                    for v in range(2):
+                        nc.tensor.transpose(
+                            flipped[:, a, v, :],
+                            words[:, 2 * pair + a, v * P : (v + 1) * P],
+                            ident[:],
+                        )
+                copy(
+                    out=grouped_words[:, 2 * pair : 2 * pair + 2, :, :],
+                    in_=flipped[:].rearrange("q a v r -> q a r v"),
+                )
+            return grouped
+
+        def group_channels(copy, by_four, name):
+            grouped = new_grouped(name)
+            copy(
+                out=grouped[:].rearrange("p (c i) j -> p c j i", i=4),
+                in_=by_four[:].rearrange("p j (c i) -> p c j i", i=4),
+            )
+            return grouped
+
+        products = {}
+
+        def diffusion_passes(b, s):
+            x1T_codes, x1T_scales = mx["x1T%d%d" % (b, s)]
+            supportT_codes, supportT_scales = mx["supportT%d" % s]
+            products[b, s] = []
+            for r in range(NODE_TILES):
+                nodes = slice(r * P, (r + 1) * P)
+                product = psum.tile([P, PACK, P], F32, tag="bank")
+                for j in range(PACK):
+                    channels = slice(j * P, (j + 1) * P)
+                    nc.tensor.matmul_mx(
+                        out=product[:, j, :],
+                        lhsT=x1T_codes[:, channels].bitcast(FP8X4),
+                        lhsT_scale=x1T_scales[:, channels],
+                        rhs=supportT_codes[:, nodes].bitcast(FP8X4),
+                        rhs_scale=supportT_scales[:, nodes],
+                        start=True,
+                        stop=True,
+                    )
+                products[b, s].append(product)
+
+        supportT0_grouped = nodes_to_partitions(support_sb[0], "supportT0", nc.vector.tensor_copy)
+        quantise("supportT0", supportT0_grouped)
+        x1T00_grouped = nodes_to_partitions(x1_sb[0, 0], "x1T00", nc.vector.tensor_copy)
+        x0_grouped = {0: group_channels(nc.vector.tensor_copy, x0_sb[0], "h00")}
+        quantise("x1T00", x1T00_grouped)
+        quantise("h00", x0_grouped[0])
+
+        waiting = []
+        waiting.append(("supportT1", nodes_to_partitions(support_sb[1], "supportT1", nc.scalar.copy)))
+        diffusion_passes(0, 0)
+        for b, s in STEPS[1:]:
+            name = "x1T%d%d" % (b, s)
+            waiting.append((name, nodes_to_partitions(x1_sb[b, s], name, nc.scalar.copy)))
+        x0_grouped[1] = group_channels(nc.scalar.copy, x0_sb[1], "h10")
+        waiting.append(("h10", x0_grouped[1]))
+        for b, s in STEPS:
+            name = "h%d%d" % (b, X1_BLOCK[s])
+            waiting.append((name, group_channels(nc.scalar.copy, x1_sb[b, s], name)))
+
+        def quantise_waiting(name, grouped):
+            quantise(name, grouped)
+            for b, s in STEPS:
+                if name == "x1T%d%d" % (b, s):
+                    diffusion_passes(b, s)
+
+        for k, (b, s) in enumerate(STEPS):
+            name = "h%d%d" % (b, X2_BLOCK[s])
+            x2_grouped = new_grouped(name)
+            for r in range(NODE_TILES):
+                nodes = slice(r * P, (r + 1) * P)
+                nc.vector.scalar_tensor_tensor(
+                    out=x2_grouped[:, nodes, :],
+                    in0=products[b, s][r][:].rearrange("p j n -> p n j"),
+                    scalar=2.0,
+                    in1=x0_grouped[b][:, nodes, :],
+                    op0=ALU.mult,
+                    op1=ALU.subtract,
+                )
+                if r % 2 == 1:
+                    quantise_waiting(*waiting[2 * k + r // 2])
+            quantise(name, x2_grouped)
+        for name, grouped in waiting[2 * len(STEPS) :]:
+            quantise_waiting(name, grouped)
+
+        kept = {}
+        for b in range(BATCH):
+            kept[b] = keep.tile([P, HID_TILES, NODES], F32, name="kept%d" % b)
+            nc.vector.tensor_tensor(out=kept[b][:], in0=u_sb[b][:], in1=hx_sb[b][:], op=ALU.mult)
+
+        for b in range(BATCH):
+            sums = [psum.tile([P, NODES], F32, tag="bank", name="sums") for i in range(HID_TILES)]
+            for g in BLOCK_ORDER:
+                h_codes, h_scales = mx["h%d%d" % (b, g)]
+                for i in range(HID_TILES):
+                    units = slice(i * P, (i + 1) * P)
+                    nc.tensor.matmul_mx(
+                        out=sums[i][:],
+                        lhsT=w_codes[:, g, units].bitcast(FP8X4),
+                        lhsT_scale=w_scales[:, g, units],
+                        rhs=h_codes[:].bitcast(FP8X4),
+                        rhs_scale=h_scales[:],
+                        start=(g == BLOCK_ORDER[0]),
+                        stop=(g == BLOCK_ORDER[-1]),
+                    )
+
+            minus_fresh = []
+            for i in range(HID_TILES):
+                cand = blend_pool.tile([P, NODES], F32)
+                nc.scalar.activation(
+                    out=cand[:], in_=sums[i][:], func=ACT.Tanh, bias=bias[:, i : i + 1], scale=1.0
+                )
+                scaled = blend_pool.tile([P, NODES], F32)
+                nc.vector.scalar_tensor_tensor(
+                    out=scaled[:],
+                    in0=u_sb[b][:, i, :],
+                    scalar=1.0,
+                    in1=cand[:],
+                    op0=ALU.subtract,
+                    op1=ALU.mult,
+                )
+                minus_fresh.append(scaled)
+            for i in range(HID_TILES):
+                result = blend_pool.tile([P, NODES], F32)
+                nc.vector.tensor_tensor(
+                    out=result[:], in0=kept[b][:, i, :], in1=minus_fresh[i][:], op=ALU.subtract
+                )
+                nc.sync.dma_start(out=out[b, i * P : (i + 1) * P, :], in_=result[:])

@@ -211,7 +211,10 @@ def tile_dcgrucell_pc_kernel(
         kept = {}
         for b in range(BATCH):
             kept[b] = keep.tile([P, HID_TILES, NODES], F32, name="kept%d" % b)
-            nc.vector.tensor_tensor(out=kept[b][:], in0=u_sb[b][:], in1=hx_sb[b][:], op=ALU.mult)
+            for i in range(HID_TILES):
+                nc.gpsimd.tensor_tensor(
+                    out=kept[b][:, i, :], in0=u_sb[b][:, i, :], in1=hx_sb[b][:, i, :], op=ALU.mult
+                )
 
         for b in range(BATCH):
             sums = [psum.tile([P, NODES], F32, tag="bank", name="sums") for i in range(HID_TILES)]

@@ -21,8 +21,8 @@ NODE_TILES = NODES // P
 HID = 384
 HID_TILES = HID // P
 BLOCKS = 5
-X_CAND, X1_BLOCK, X2_BLOCK = 0, (1, 3), (2, 4)
-BLOCK_ORDER = (0, 2, 4, 1, 3)
+X_CAND = 0
+X2_BLOCK = (2, 4)
 STEPS = tuple((b, s) for b in range(BATCH) for s in range(2))
 
 FLOPS = 2 * 2 * BATCH * CHANNELS * NODES * NODES + 2 * BATCH * BLOCKS * CHANNELS * HID * NODES
@@ -38,7 +38,6 @@ def tile_dcgrucell_pc_kernel(
     with ExitStack() as ctx:
         ctx.enter_context(tc.manual_schedule())
         keep = ctx.enter_context(tc.tile_pool(name="keep", bufs=1))
-        blend_pool = ctx.enter_context(tc.tile_pool(name="blend_pool", bufs=HID_TILES))
         psum = ctx.enter_context(tc.psum_pool(name="psum", bufs=8))
 
         w_scales = keep.tile([P, BLOCKS, HID], U8, align_bytes=64)
@@ -80,17 +79,26 @@ def tile_dcgrucell_pc_kernel(
         x0_sb[0] = load_channels(x_cand[0], "x0_sb0")
         support_sb[1] = load_support(1)
         x1_sb[0, 1] = load_channels(x1[1][0], "x1_sb01")
+        u_sb[0] = load_hidden(u[0], "u_sb0")
+        hx_sb[0] = load_hidden(hx[0], "hx_sb0")
         x1_sb[1, 0] = load_channels(x1[0][1], "x1_sb10")
-        x1_sb[1, 1] = load_channels(x1[1][1], "x1_sb11")
         x0_sb[1] = load_channels(x_cand[1], "x0_sb1")
+        x1_sb[1, 1] = load_channels(x1[1][1], "x1_sb11")
         w_codes = keep.tile([P, BLOCKS, HID], U32, align_bytes=64)
         nc.sync.dma_start(
             out=w_codes[:].bitcast(I32),
             in_=W_c_words.rearrange("g p o t -> p g (o t)").bitcast(I32),
         )
+        u_sb[1] = load_hidden(u[1], "u_sb1")
+        hx_sb[1] = load_hidden(hx[1], "hx_sb1")
+
+        kept = {}
         for b in range(BATCH):
-            u_sb[b] = load_hidden(u[b], "u_sb%d" % b)
-            hx_sb[b] = load_hidden(hx[b], "hx_sb%d" % b)
+            kept[b] = keep.tile([P, HID_TILES, NODES], F32, name="kept%d" % b)
+            for i in range(HID_TILES):
+                nc.gpsimd.tensor_tensor(
+                    out=kept[b][:, i, :], in0=u_sb[b][:, i, :], in1=hx_sb[b][:, i, :], op=ALU.mult
+                )
 
         bias_rows = keep.tile([P, P], F32)
         nc.vector.memset(bias_rows[:], 0.0)
@@ -100,25 +108,28 @@ def tile_dcgrucell_pc_kernel(
         bias = keep.tile([P, HID_TILES], F32)
         nc.vector.tensor_copy(out=bias[:], in_=bias_bank[:, 0:HID_TILES])
 
+        grouped = {}
         mx = {}
 
         def new_grouped(name):
-            return keep.tile([P, NODES, PACK], BF16, name=name + "_grouped", align_bytes=64)
+            grouped[name] = keep.tile(
+                [P, NODES, PACK], BF16, name=name + "_grouped", align_bytes=64
+            )
+            return grouped[name]
 
-        def quantise(name, grouped):
+        def quantise(name):
             codes = keep.tile([P, NODES], U32, name=name + "_codes", align_bytes=64)
             scales = keep.tile([P, NODES], U8, name=name + "_scales", align_bytes=64)
             nc.vector.quantize_mx(
                 out=codes[:].bitcast(FP8X4),
                 scales=scales[:],
-                in_=grouped[:].rearrange("p c t -> p (c t)"),
+                in_=grouped[name][:].rearrange("p c t -> p (c t)"),
             )
             mx[name] = (codes, scales)
 
-        def nodes_to_partitions(rows_sb, name, second_copy):
+        def nodes_to_partitions(name, rows_sb, second_copy=nc.scalar.copy):
             words = rows_sb[:].bitcast(F32)
-            grouped = new_grouped(name)
-            grouped_words = grouped[:].bitcast(F32).rearrange("q (a r) v -> q a r v", r=P)
+            grouped_words = new_grouped(name)[:].bitcast(F32).rearrange("q (a r) v -> q a r v", r=P)
             for pair, copy in enumerate((nc.scalar.copy, second_copy)):
                 flipped = psum.tile([P, 2, 2, P], F32, tag="bank")
                 for a in range(2):
@@ -132,15 +143,12 @@ def tile_dcgrucell_pc_kernel(
                     out=grouped_words[:, 2 * pair : 2 * pair + 2, :, :],
                     in_=flipped[:].rearrange("q a v r -> q a r v"),
                 )
-            return grouped
 
-        def group_channels(copy, by_four, name):
-            grouped = new_grouped(name)
+        def group_channels(name, by_four, copy=nc.scalar.copy):
             copy(
-                out=grouped[:].rearrange("p (c i) j -> p c j i", i=4),
+                out=new_grouped(name)[:].rearrange("p (c i) j -> p c j i", i=4),
                 in_=by_four[:].rearrange("p j (c i) -> p c j i", i=4),
             )
-            return grouped
 
         products = {}
 
@@ -164,81 +172,88 @@ def tile_dcgrucell_pc_kernel(
                     )
                 products[b, s].append(product)
 
-        supportT0_grouped = nodes_to_partitions(support_sb[0], "supportT0", nc.vector.tensor_copy)
-        quantise("supportT0", supportT0_grouped)
-        x1T00_grouped = nodes_to_partitions(x1_sb[0, 0], "x1T00", nc.vector.tensor_copy)
-        x0_grouped = {0: group_channels(nc.vector.tensor_copy, x0_sb[0], "h00")}
-        quantise("x1T00", x1T00_grouped)
-        quantise("h00", x0_grouped[0])
+        sums = {}
+        mixed = {b: [] for b in range(BATCH)}
 
-        waiting = []
-        waiting.append(("supportT1", nodes_to_partitions(support_sb[1], "supportT1", nc.scalar.copy)))
+        def mixing_passes(b, g):
+            if not mixed[b]:
+                sums[b] = [
+                    psum.tile([P, NODES], F32, tag="bank", name="sums") for i in range(HID_TILES)
+                ]
+            mixed[b].append(g)
+            h_codes, h_scales = mx["h%d%d" % (b, g)]
+            for i in range(HID_TILES):
+                units = slice(i * P, (i + 1) * P)
+                nc.tensor.matmul_mx(
+                    out=sums[b][i][:],
+                    lhsT=w_codes[:, g, units].bitcast(FP8X4),
+                    lhsT_scale=w_scales[:, g, units],
+                    rhs=h_codes[:].bitcast(FP8X4),
+                    rhs_scale=h_scales[:],
+                    start=(len(mixed[b]) == 1),
+                    stop=(len(mixed[b]) == BLOCKS),
+                )
+
+        nodes_to_partitions("supportT0", support_sb[0], nc.vector.tensor_copy)
+        quantise("supportT0")
+        nodes_to_partitions("x1T00", x1_sb[0, 0], nc.vector.tensor_copy)
+        group_channels("h00", x0_sb[0], nc.vector.tensor_copy)
+        quantise("x1T00")
+        quantise("h00")
+        quantised_blocks = [(0, X_CAND)]
+
+        group_channels("h01", x1_sb[0, 0])
+        nodes_to_partitions("supportT1", support_sb[1])
         diffusion_passes(0, 0)
-        for b, s in STEPS[1:]:
-            name = "x1T%d%d" % (b, s)
-            waiting.append((name, nodes_to_partitions(x1_sb[b, s], name, nc.scalar.copy)))
-        x0_grouped[1] = group_channels(nc.scalar.copy, x0_sb[1], "h10")
-        waiting.append(("h10", x0_grouped[1]))
-        for b, s in STEPS:
-            name = "h%d%d" % (b, X1_BLOCK[s])
-            waiting.append((name, group_channels(nc.scalar.copy, x1_sb[b, s], name)))
+        nodes_to_partitions("x1T01", x1_sb[0, 1])
+        nodes_to_partitions("x1T10", x1_sb[1, 0])
+        group_channels("h03", x1_sb[0, 1])
+        group_channels("h10", x0_sb[1])
+        input_blocks = [(0, 1), (0, 3), (1, 0), (1, 1), (1, 3)]
 
-        def quantise_waiting(name, grouped):
-            quantise(name, grouped)
-            for b, s in STEPS:
-                if name == "x1T%d%d" % (b, s):
-                    diffusion_passes(b, s)
-
+        passes_issued = 0
         for k, (b, s) in enumerate(STEPS):
-            name = "h%d%d" % (b, X2_BLOCK[s])
-            x2_grouped = new_grouped(name)
+            x2_grouped = new_grouped("h%d%d" % (b, X2_BLOCK[s]))
             for r in range(NODE_TILES):
                 nodes = slice(r * P, (r + 1) * P)
                 nc.vector.scalar_tensor_tensor(
                     out=x2_grouped[:, nodes, :],
                     in0=products[b, s][r][:].rearrange("p j n -> p n j"),
                     scalar=2.0,
-                    in1=x0_grouped[b][:, nodes, :],
+                    in1=grouped["h%d%d" % (b, X_CAND)][:, nodes, :],
                     op0=ALU.mult,
                     op1=ALU.subtract,
                 )
-                if r % 2 == 1:
-                    quantise_waiting(*waiting[2 * k + r // 2])
-            quantise(name, x2_grouped)
-        for name, grouped in waiting[2 * len(STEPS) :]:
-            quantise_waiting(name, grouped)
+            for next_b, next_s in STEPS[k + 1 : k + 2]:
+                if next_b == 0:
+                    quantise("supportT%d" % next_s)
+                quantise("x1T%d%d" % (next_b, next_s))
+                diffusion_passes(next_b, next_s)
+            if k > 0:
+                for block in quantised_blocks[passes_issued:]:
+                    mixing_passes(*block)
+                passes_issued = len(quantised_blocks)
+            for block in ((b, X2_BLOCK[s]), input_blocks[k]):
+                quantise("h%d%d" % block)
+                quantised_blocks.append(block)
+            if k == 0:
+                nodes_to_partitions("x1T11", x1_sb[1, 1])
+                group_channels("h11", x1_sb[1, 0])
+                group_channels("h13", x1_sb[1, 1])
+        for block in input_blocks[len(STEPS) :]:
+            quantise("h%d%d" % block)
+            quantised_blocks.append(block)
+        for block in quantised_blocks[passes_issued:]:
+            mixing_passes(*block)
 
-        kept = {}
         for b in range(BATCH):
-            kept[b] = keep.tile([P, HID_TILES, NODES], F32, name="kept%d" % b)
-            for i in range(HID_TILES):
-                nc.gpsimd.tensor_tensor(
-                    out=kept[b][:, i, :], in0=u_sb[b][:, i, :], in1=hx_sb[b][:, i, :], op=ALU.mult
-                )
-
-        for b in range(BATCH):
-            sums = [psum.tile([P, NODES], F32, tag="bank", name="sums") for i in range(HID_TILES)]
-            for g in BLOCK_ORDER:
-                h_codes, h_scales = mx["h%d%d" % (b, g)]
-                for i in range(HID_TILES):
-                    units = slice(i * P, (i + 1) * P)
-                    nc.tensor.matmul_mx(
-                        out=sums[i][:],
-                        lhsT=w_codes[:, g, units].bitcast(FP8X4),
-                        lhsT_scale=w_scales[:, g, units],
-                        rhs=h_codes[:].bitcast(FP8X4),
-                        rhs_scale=h_scales[:],
-                        start=(g == BLOCK_ORDER[0]),
-                        stop=(g == BLOCK_ORDER[-1]),
-                    )
-
             minus_fresh = []
             for i in range(HID_TILES):
-                cand = blend_pool.tile([P, NODES], F32)
+                cand = keep.tile([P, NODES], F32, name="cand%d%d" % (b, i))
                 nc.scalar.activation(
-                    out=cand[:], in_=sums[i][:], func=ACT.Tanh, bias=bias[:, i : i + 1], scale=1.0
+                    out=cand[:], in_=sums[b][i][:], func=ACT.Tanh, bias=bias[:, i : i + 1], scale=1.0
                 )
-                scaled = blend_pool.tile([P, NODES], F32)
+                scaled = keep.tile([P, NODES], F32, name="scaled%d%d" % (b, i))
                 nc.vector.scalar_tensor_tensor(
                     out=scaled[:],
                     in0=u_sb[b][:, i, :],
@@ -249,7 +264,7 @@ def tile_dcgrucell_pc_kernel(
                 )
                 minus_fresh.append(scaled)
             for i in range(HID_TILES):
-                result = blend_pool.tile([P, NODES], F32)
+                result = keep.tile([P, NODES], F32, name="result%d%d" % (b, i))
                 nc.vector.tensor_tensor(
                     out=result[:], in0=kept[b][:, i, :], in1=minus_fresh[i][:], op=ALU.subtract
                 )

from contextlib import ExitStack

import concourse.mybir as mybir
from concourse.masks import make_identity

F32 = mybir.dt.float32
BF16 = mybir.dt.bfloat16
I32 = mybir.dt.int32
U32 = mybir.dt.uint32
U8 = mybir.dt.uint8
FP8X4 = mybir.dt.float8_e4m3fn_x4
ALU = mybir.AluOpType
ACT = mybir.ActivationFunctionType

P = 128
PACK = 4
BATCH = 2
CHANNELS = P * PACK
NODES = 512
NODE_TILES = NODES // P
HID = 384
HID_TILES = HID // P
BLOCKS = 5
X_CAND = 0
X2_BLOCK = (2, 4)
STEPS = tuple((b, s) for b in range(BATCH) for s in range(2))

FLOPS = 2 * 2 * BATCH * CHANNELS * NODES * NODES + 2 * BATCH * BLOCKS * CHANNELS * HID * NODES


def tile_dcgrucell_pc_kernel(
    tc, x_cand, x1_0, x1_1, support0, support1, W_c_words, W_c_scales, b_c, u, hx, out
):
    nc = tc.nc
    x1 = (x1_0, x1_1)
    support = (support0, support1)

    with ExitStack() as ctx:
        ctx.enter_context(tc.manual_schedule())
        keep = ctx.enter_context(tc.tile_pool(name="keep", bufs=1))
        psum = ctx.enter_context(tc.psum_pool(name="psum", bufs=8))

        w_scales = keep.tile([P, BLOCKS, HID], U8, align_bytes=64)
        nc.vector.memset(w_scales[:].rearrange("p g o -> p (g o)").bitcast(I32), 0)
        ident = keep.tile([P, P], F32)
        make_identity(nc, ident[:])
        for quadrant in range(4):
            nc.gpsimd.dma_start(
                out=w_scales[32 * quadrant : 32 * quadrant + 4, :, :].bitcast(F32),
                in_=W_c_scales[:, 4 * quadrant : 4 * quadrant + 4, :]
                .rearrange("g r o -> r g o")
                .bitcast(F32),
            )
        zero_column = keep.tile([P, 1], F32)
        nc.vector.memset(zero_column[:], 0.0)
        table_warmer = keep.tile([P, 1], F32)
        nc.scalar.activation(out=table_warmer[:], in_=zero_column[:], func=ACT.Tanh)

        def load_channels(src, name):
            by_four = keep.tile([P, PACK, NODES], BF16, name=name)
            nc.sync.dma_start(out=by_four[:], in_=src.rearrange("(p j) n -> p j n", j=PACK))
            return by_four

        def load_support(s):
            rows = keep.tile([P, NODE_TILES, NODES], BF16, name="support_sb%d" % s)
            nc.sync.dma_start(out=rows[:], in_=support[s].rearrange("(r p) n -> p r n", p=P))
            return rows

        def load_hidden(src, name):
            rows = keep.tile([P, HID_TILES, NODES], BF16, name=name)
            nc.sync.dma_start(out=rows[:], in_=src.rearrange("(i p) n -> p i n", p=P))
            return rows

        bias_bf16 = keep.tile([HID_TILES, P], BF16)
        nc.sync.dma_start(out=bias_bf16[:], in_=b_c.rearrange("(i p) -> i p", p=P))
        support_sb, x0_sb, x1_sb, u_sb, hx_sb = {}, {}, {}, {}, {}
        support_sb[0] = load_support(0)
        x1_sb[0, 0] = load_channels(x1[0][0], "x1_sb00")
        x0_sb[0] = load_channels(x_cand[0], "x0_sb0")
        support_sb[1] = load_support(1)
        x1_sb[0, 1] = load_channels(x1[1][0], "x1_sb01")
        u_sb[0] = load_hidden(u[0], "u_sb0")
        hx_sb[0] = load_hidden(hx[0], "hx_sb0")
        x1_sb[1, 0] = load_channels(x1[0][1], "x1_sb10")
        x0_sb[1] = load_channels(x_cand[1], "x0_sb1")
        x1_sb[1, 1] = load_channels(x1[1][1], "x1_sb11")
        w_codes = keep.tile([P, BLOCKS, HID], U32, align_bytes=64)
        nc.sync.dma_start(
            out=w_codes[:].bitcast(I32),
            in_=W_c_words.rearrange("g p o t -> p g (o t)").bitcast(I32),
        )
        u_sb[1] = load_hidden(u[1], "u_sb1")
        hx_sb[1] = load_hidden(hx[1], "hx_sb1")

        kept = {}
        for b in range(BATCH):
            kept[b] = keep.tile([P, HID_TILES, NODES], F32, name="kept%d" % b)
            for i in range(HID_TILES):
                nc.gpsimd.tensor_tensor(
                    out=kept[b][:, i, :], in0=u_sb[b][:, i, :], in1=hx_sb[b][:, i, :], op=ALU.mult
                )

        bias_rows = keep.tile([P, P], F32)
        nc.vector.memset(bias_rows[:], 0.0)
        nc.vector.tensor_copy(out=bias_rows[0:HID_TILES, :], in_=bias_bf16[:])
        bias_bank = psum.tile([P, P], F32, tag="bank")
        nc.tensor.transpose(bias_bank[:], bias_rows[:], ident[:])
        bias = keep.tile([P, HID_TILES], F32)
        nc.vector.tensor_copy(out=bias[:], in_=bias_bank[:, 0:HID_TILES])

        grouped = {}
        mx = {}

        def new_grouped(name):
            grouped[name] = keep.tile(
                [P, NODES, PACK], BF16, name=name + "_grouped", align_bytes=64
            )
            return grouped[name]

        def quantise(name):
            codes = keep.tile([P, NODES], U32, name=name + "_codes", align_bytes=64)
            scales = keep.tile([P, NODES], U8, name=name + "_scales", align_bytes=64)
            nc.vector.quantize_mx(
                out=codes[:].bitcast(FP8X4),
                scales=scales[:],
                in_=grouped[name][:].rearrange("p c t -> p (c t)"),
            )
            mx[name] = (codes, scales)

        def nodes_to_partitions(name, rows_sb, second_copy=nc.scalar.copy):
            words = rows_sb[:].bitcast(F32)
            grouped_words = new_grouped(name)[:].bitcast(F32).rearrange("q (a r) v -> q a r v", r=P)
            for pair, copy in enumerate((nc.scalar.copy, second_copy)):
                flipped = psum.tile([P, 2, 2, P], F32, tag="bank")
                for a in range(2):
                    for v in range(2):
                        nc.tensor.transpose(
                            flipped[:, a, v, :],
                            words[:, 2 * pair + a, v * P : (v + 1) * P],
                            ident[:],
                        )
                copy(
                    out=grouped_words[:, 2 * pair : 2 * pair + 2, :, :],
                    in_=flipped[:].rearrange("q a v r -> q a r v"),
                )

        def group_channels(name, by_four, copy=nc.scalar.copy):
            copy(
                out=new_grouped(name)[:].rearrange("p (c i) j -> p c j i", i=4),
                in_=by_four[:].rearrange("p j (c i) -> p c j i", i=4),
            )

        products = {}

        def diffusion_passes(b, s):
            x1T_codes, x1T_scales = mx["x1T%d%d" % (b, s)]
            supportT_codes, supportT_scales = mx["supportT%d" % s]
            products[b, s] = []
            for r in range(NODE_TILES):
                nodes = slice(r * P, (r + 1) * P)
                product = psum.tile([P, PACK, P], F32, tag="bank")
                for j in range(PACK):
                    channels = slice(j * P, (j + 1) * P)
                    nc.tensor.matmul_mx(
                        out=product[:, j, :],
                        lhsT=x1T_codes[:, channels].bitcast(FP8X4),
                        lhsT_scale=x1T_scales[:, channels],
                        rhs=supportT_codes[:, nodes].bitcast(FP8X4),
                        rhs_scale=supportT_scales[:, nodes],
                        start=True,
                        stop=True,
                    )
                products[b, s].append(product)

        sums = {}
        mixed = {b: [] for b in range(BATCH)}

        def mixing_passes(b, g):
            if not mixed[b]:
                sums[b] = [
                    psum.tile([P, NODES], F32, tag="bank", name="sums") for i in range(HID_TILES)
                ]
            mixed[b].append(g)
            h_codes, h_scales = mx["h%d%d" % (b, g)]
            for i in range(HID_TILES):
                units = slice(i * P, (i + 1) * P)
                nc.tensor.matmul_mx(
                    out=sums[b][i][:],
                    lhsT=w_codes[:, g, units].bitcast(FP8X4),
                    lhsT_scale=w_scales[:, g, units],
                    rhs=h_codes[:].bitcast(FP8X4),
                    rhs_scale=h_scales[:],
                    start=(len(mixed[b]) == 1),
                    stop=(len(mixed[b]) == BLOCKS),
                )

        nodes_to_partitions("supportT0", support_sb[0], nc.vector.tensor_copy)
        quantise("supportT0")
        nodes_to_partitions("x1T00", x1_sb[0, 0], nc.vector.tensor_copy)
        group_channels("h00", x0_sb[0], nc.vector.tensor_copy)
        quantise("x1T00")
        quantise("h00")
        quantised_blocks = [(0, X_CAND)]

        group_channels("h01", x1_sb[0, 0])
        nodes_to_partitions("supportT1", support_sb[1])
        diffusion_passes(0, 0)
        nodes_to_partitions("x1T01", x1_sb[0, 1])
        nodes_to_partitions("x1T10", x1_sb[1, 0])
        group_channels("h03", x1_sb[0, 1])
        group_channels("h10", x0_sb[1])
        input_blocks = [(0, 1), (0, 3), (1, 0), (1, 1), (1, 3)]

        passes_issued = 0
        for k, (b, s) in enumerate(STEPS):
            x2_grouped = new_grouped("h%d%d" % (b, X2_BLOCK[s]))
            for r in range(NODE_TILES):
                nodes = slice(r * P, (r + 1) * P)
                nc.vector.scalar_tensor_tensor(
                    out=x2_grouped[:, nodes, :],
                    in0=products[b, s][r][:].rearrange("p j n -> p n j"),
                    scalar=2.0,
                    in1=grouped["h%d%d" % (b, X_CAND)][:, nodes, :],
                    op0=ALU.mult,
                    op1=ALU.subtract,
                )
            for next_b, next_s in STEPS[k + 1 : k + 2]:
                if next_b == 0:
                    quantise("supportT%d" % next_s)
                quantise("x1T%d%d" % (next_b, next_s))
                diffusion_passes(next_b, next_s)
            if k > 0:
                for block in quantised_blocks[passes_issued:]:
                    mixing_passes(*block)
                passes_issued = len(quantised_blocks)
            for block in ((b, X2_BLOCK[s]), input_blocks[k]):
                quantise("h%d%d" % block)
                quantised_blocks.append(block)
            if k == 0:
                nodes_to_partitions("x1T11", x1_sb[1, 1])
                group_channels("h11", x1_sb[1, 0])
                group_channels("h13", x1_sb[1, 1])
        for block in input_blocks[len(STEPS) :]:
            quantise("h%d%d" % block)
            quantised_blocks.append(block)
        for block in quantised_blocks[passes_issued:]:
            mixing_passes(*block)

        for b in range(BATCH):
            minus_fresh = []
            for i in range(HID_TILES):
                cand = keep.tile([P, NODES], F32, name="cand%d%d" % (b, i))
                nc.scalar.activation(
                    out=cand[:], in_=sums[b][i][:], func=ACT.Tanh, bias=bias[:, i : i + 1], scale=1.0
                )
                scaled = keep.tile([P, NODES], F32, name="scaled%d%d" % (b, i))
                nc.vector.scalar_tensor_tensor(
                    out=scaled[:],
                    in0=u_sb[b][:, i, :],
                    scalar=1.0,
                    in1=cand[:],
                    op0=ALU.subtract,
                    op1=ALU.mult,
                )
                minus_fresh.append(scaled)
            for i in range(HID_TILES):
                result = keep.tile([P, NODES], F32, name="result%d%d" % (b, i))
                nc.vector.tensor_tensor(
                    out=result[:], in0=kept[b][:, i, :], in1=minus_fresh[i][:], op=ALU.subtract
                )
                nc.sync.dma_start(out=out[b, i * P : (i + 1) * P, :], in_=result[:])
